import numpy as np
import ml_dtypes


def mxq(x, axis, fmt="e4m3"):
    dtype, down = {"e4m3": (ml_dtypes.float8_e4m3fn, 7), "e5m2": (ml_dtypes.float8_e5m2, 14)}[fmt]
    v = np.moveaxis(np.asarray(x, np.float32).astype(ml_dtypes.bfloat16).astype(np.float64), axis, -1)
    blocks = v.reshape(v.shape[:-1] + (-1, 32))
    amax = np.abs(blocks).max(-1, keepdims=True)
    byte = np.maximum(np.where(amax > 0, np.frexp(amax)[1] - 1 + 127, 0) - down, 1)
    scale = np.exp2(byte - 127.0)
    codes = (blocks / scale).astype(np.float32).astype(dtype).astype(np.float64)
    return np.moveaxis((codes * scale).reshape(v.shape), -1, axis)


WIDE = False


def mx_kscale(k):
    if not WIDE:
        return np.ones(k)
    levels = np.array([10, -10, 5, -5, 0])
    a = np.random.permutation(np.resize(levels, k // 512 * 4)).reshape(k // 512, 4)
    idx = np.arange(k)
    return np.exp2(a[idx // 512, idx % 128 // 32])


BF16 = ml_dtypes.bfloat16


def bf(x):
    return np.asarray(x, np.float32).astype(BF16)


def f64(x):
    return np.asarray(x).astype(np.float64)


E2M1 = np.array([0.0, 0.5, 1.0, 1.5, 2.0, 3.0, 4.0, 6.0, -0.0, -0.5, -1.0, -1.5, -2.0, -3.0, -4.0, -6.0])


def pack_weight(w, fmt):
    k, n = w.shape
    w = f64(bf(w)).reshape(k // 32, 32, n)
    amax = np.abs(w).max(1)
    if fmt == "e4m3":
        byte = np.frexp(amax)[1] - 1 + 127 - 7
    else:
        mant, ex = np.frexp(amax / 6.0)
        byte = np.where(mant > 0.5, ex, ex - 1) + 127
    byte = np.clip(np.where(amax > 0, byte, 1), 1, 254)
    scaled = (w * np.exp2(127.0 - byte)[:, None, :]).reshape(k, n).astype(np.float32)
    by_word = np.ascontiguousarray(scaled.reshape(k // 512, 128, 4, n).transpose(0, 1, 3, 2))
    if fmt == "e4m3":
        words = by_word.astype(ml_dtypes.float8_e4m3fn).view(np.uint8)
    else:
        c = by_word.astype(ml_dtypes.float4_e2m1fn).view(np.uint8) & 0xF
        words = c[..., 0::2] | (c[..., 1::2] << 4)
    return np.ascontiguousarray(words), np.ascontiguousarray(byte.astype(np.uint8).reshape(k // 512, 16, n))


def unpack_weight(words, scales, fmt):
    g, p, n, _ = words.shape
    if fmt == "e4m3":
        vals = np.ascontiguousarray(words).view(ml_dtypes.float8_e4m3fn).astype(np.float64)
    else:
        nib = np.empty((g, p, n, 4), np.uint8)
        nib[..., 0::2] = words & 0xF
        nib[..., 1::2] = words >> 4
        vals = E2M1[nib]
    vals = vals * np.repeat(np.exp2(scales.astype(np.float64) - 127.0), 8, axis=1)[..., None]
    return vals.transpose(0, 1, 3, 2).reshape(g * 512, n)

def pack4(w):
    words, scales = pack_weight(w, "e2m1")
    return words.reshape(words.shape[0], 128, -1), scales


def unpack4(words, scales):
    return unpack_weight(words.reshape(words.shape[0], 128, -1, 2), scales, "e2m1")


B, S, D, H, DK = 4, 2048, 1024, 1, 128
E = H * DK
HALF = DK // 2


def rope(t, cos2, sin2):
    t_even = t[..., 0::2]
    t_odd = t[..., 1::2]
    rot = np.stack([-t_odd, t_even], axis=-1).reshape(t.shape)
    return t * cos2 + rot * sin2


def setup_inputs():
    s = mx_kscale(D)
    ang = np.random.uniform(-np.pi, np.pi, (S, HALF))
    x = bf(np.random.standard_normal((B, S, D)) * s)
    Wq_words, Wq_scales = pack4(np.random.standard_normal((D, E)) / np.sqrt(D) / s[:, None])
    Wk_words, Wk_scales = pack4(np.random.standard_normal((D, E)) / np.sqrt(D) / s[:, None])
    return {"x": x,
            "Wq_words": Wq_words,
            "Wq_scales": Wq_scales,
            "Wk_words": Wk_words,
            "Wk_scales": Wk_scales,
            "cos2": bf(np.repeat(np.cos(ang), 2, axis=-1)),
            "sin2": bf(np.repeat(np.sin(ang), 2, axis=-1))}


def reference(x, Wq_words, Wq_scales, Wk_words, Wk_scales, cos2, sin2):
    xq = mxq(f64(x), 2, "e4m3")
    q = (xq @ unpack4(Wq_words, Wq_scales)).reshape(B, S, H, DK).swapaxes(1, 2)
    k = (xq @ unpack4(Wk_words, Wk_scales)).reshape(B, S, H, DK).swapaxes(1, 2)
    c, sn = f64(cos2), f64(sin2)
    return rope(q, c, sn), rope(k, c, sn)

@@ -1,0 +1,212 @@
+from contextlib import ExitStack
+
+import concourse.mybir as mybir
+from concourse.masks import make_identity
+
+F32 = mybir.dt.float32
+BF16 = mybir.dt.bfloat16
+I32 = mybir.dt.int32
+U32 = mybir.dt.uint32
+U8 = mybir.dt.uint8
+FP8X4 = mybir.dt.float8_e4m3fn_x4
+FP4X4 = mybir.dt.float4_e2m1fn_x4
+MULT = mybir.AluOpType.mult
+ADD = mybir.AluOpType.add
+
+P = 128
+BATCH = 4
+SEQ = 2048
+D_MODEL = 1024
+HEAD = 128
+K_PASS = 4 * P
+PASSES = D_MODEL // K_PASS
+ROWS = SEQ // P
+TILES = 4
+CHUNKS = BATCH * ROWS // TILES
+AHEAD = 8
+PLANE = ROWS * HEAD
+NEG_SIN = 0
+COS = 1
+SIN = 2
+BANK = 512
+
+FLOPS = 2 * BATCH * SEQ * D_MODEL * 2 * HEAD
+
+
+def tile_multiheadselfattention_pa_t_kernel(
+    tc, x, Wq_words, Wq_scales, Wk_words, Wk_scales, cos2, sin2, out_0, out_1
+):
+    nc = tc.nc
+    outs = [out_0, out_1]
+
+    with ExitStack() as stack:
+        const = stack.enter_context(tc.tile_pool(name="const", bufs=1))
+        x_pool = stack.enter_context(tc.tile_pool(name="x", bufs=AHEAD))
+        grouped_pool = stack.enter_context(tc.tile_pool(name="grouped", bufs=2))
+        mx_pool = stack.enter_context(tc.tile_pool(name="mx", bufs=3))
+        product_pool = stack.enter_context(tc.tile_pool(name="product", bufs=4))
+        out_pool = stack.enter_context(tc.tile_pool(name="out", bufs=6))
+        flipped_pool = stack.enter_context(tc.psum_pool(name="flipped", bufs=TILES))
+        sums_pool = stack.enter_context(tc.psum_pool(name="sums", bufs=TILES))
+
+        identity = const.tile([P, P], F32)
+        make_identity(nc, identity[:])
+
+        w_words = const.tile([P, 2, PASSES, 2 * HEAD], U8, align_bytes=64)
+        w_planes = const.tile([P, 2, PASSES, HEAD], U8, align_bytes=64)
+        nc.vector.memset(w_planes[:].rearrange("p w g n -> p (w g n)").bitcast(I32), 0)
+
+        table = const.tile([P, 4 * PLANE], BF16)
+
+        x_tiles = {}
+        codes_of = {}
+        planes_of = {}
+        sums_of = {}
+
+        def place(c):
+            per_batch = ROWS // TILES
+            return c // per_batch, (c % per_batch) * TILES
+
+        def load_x(c):
+            b, row0 = place(c)
+            x_sb = x_pool.tile([P, TILES, D_MODEL], BF16)
+            rows = x[b].rearrange("(p t) k -> p t k", t=ROWS)
+            nc.sync.dma_start(out=x_sb[:], in_=rows[:, row0 : row0 + TILES, :])
+            x_tiles[c] = x_sb
+
+        def load_weight(w, words, scales):
+            nc.sync.dma_start(
+                out=w_words[:, w, :, :].bitcast(I32),
+                in_=words.bitcast(I32).rearrange("g p c -> p g c"),
+            )
+            for quadrant in range(4):
+                nc.sync.dma_start(
+                    out=w_planes[32 * quadrant : 32 * quadrant + 4, w, :, :].bitcast(I32),
+                    in_=scales.bitcast(I32)[:, 4 * quadrant : 4 * quadrant + 4, :].rearrange(
+                        "g r n -> r g n"
+                    ),
+                )
+
+        def load_table(plane, values):
+            nc.sync.dma_start(
+                out=table[:, plane * PLANE : (plane + 1) * PLANE],
+                in_=values.rearrange("(p t) d -> p (t d)", t=ROWS),
+            )
+
+        def transpose_and_group(c):
+            grouped = grouped_pool.tile([P, TILES * D_MODEL], BF16, align_bytes=64)
+            grouped_words = grouped[:].bitcast(F32)
+            for i in range(TILES):
+                words = x_tiles[c][:, i, :].bitcast(F32)
+                flipped = flipped_pool.tile([P, BANK], F32)
+                for g in range(PASSES):
+                    for u in range(2):
+                        nc.tensor.transpose(
+                            flipped[:, (2 * g + u) * P : (2 * g + u + 1) * P],
+                            words[:, 2 * P * g + u : 2 * P * (g + 1) : 2],
+                            identity[:],
+                        )
+                nc.scalar.copy(
+                    out=grouped_words[:, i * BANK : (i + 1) * BANK].rearrange(
+                        "p (g r u) -> p g r u", g=PASSES, u=2
+                    ),
+                    in_=flipped[:].rearrange("p (g u r) -> p g r u", g=PASSES, u=2),
+                )
+            return grouped
+
+        def quantise(c, grouped):
+            codes = mx_pool.tile([P, TILES * PASSES * P], U32, align_bytes=64)
+            planes = mx_pool.tile([P, TILES * PASSES * P], U8, align_bytes=64)
+            nc.vector.quantize_mx(out=codes[:].bitcast(FP8X4), scales=planes[:], in_=grouped[:])
+            codes_of[c] = codes
+            planes_of[c] = planes
+
+        def project(c):
+            sums_of[c] = []
+            for half in range(TILES // 2):
+                sums = sums_pool.tile([P, BANK], F32)
+                for w in range(2):
+                    for i in range(2):
+                        for g in range(PASSES):
+                            tokens = slice(
+                                ((2 * half + i) * PASSES + g) * P,
+                                ((2 * half + i) * PASSES + g + 1) * P,
+                            )
+                            nc.tensor.matmul_mx(
+                                out=sums[:, (2 * w + i) * HEAD : (2 * w + i + 1) * HEAD],
+                                lhsT=codes_of[c][:, tokens].bitcast(FP8X4),
+                                lhsT_scale=planes_of[c][:, tokens],
+                                rhs=w_words[:, w, g, :].bitcast(FP4X4),
+                                rhs_scale=w_planes[:, w, g, :],
+                                start=(g == 0),
+                                stop=(g == PASSES - 1),
+                            )
+                sums_of[c].append(sums)
+
+        bank_shape = [P, 2, HEAD, 2]
+
+        def factors(first, row):
+            start = first * PLANE + row * HEAD
+            window = table[:, start : start + 2 * (PLANE + 1)].rearrange("p (e n) -> p e n", e=2)
+            both = window[:, :, 0 : 2 * HEAD : 2].rearrange("p e n -> p n e")
+            return both.unsqueeze(1).to_broadcast(bank_shape)
+
+        def rotate_and_store(c):
+            b, row0 = place(c)
+            rotated = out_pool.tile([P, 2, TILES, HEAD], F32)
+            products = []
+            for half in range(TILES // 2):
+                pairs = sums_of[c][half][:].rearrange("p (w n e) -> p w n e", w=2, e=2)
+                row = row0 + 2 * half
+                from_even = product_pool.tile(bank_shape, F32)
+                nc.vector.tensor_tensor(
+                    out=from_even[:],
+                    in0=pairs[:, :, :, 0:1].to_broadcast(bank_shape),
+                    in1=factors(COS, row),
+                    op=MULT,
+                )
+                from_odd = product_pool.tile(bank_shape, F32)
+                nc.vector.tensor_tensor(
+                    out=from_odd[:],
+                    in0=pairs[:, :, :, 1:2].to_broadcast(bank_shape),
+                    in1=factors(NEG_SIN, row),
+                    op=MULT,
+                )
+                products.append((from_even, from_odd))
+            for half in range(TILES // 2):
+                from_even, from_odd = products[half]
+                nc.vector.tensor_tensor(
+                    out=rotated[:, :, 2 * half : 2 * half + 2, :].rearrange("p w i d -> p w (i d)"),
+                    in0=from_even[:].rearrange("p w n e -> p w (n e)"),
+                    in1=from_odd[:].rearrange("p w n e -> p w (n e)"),
+                    op=ADD,
+                )
+            for w in range(2):
+                rows = outs[w][b, 0].rearrange("(p t) d -> p t d", t=ROWS)
+                nc.sync.dma_start(out=rows[:, row0 : row0 + TILES, :], in_=rotated[:, w, :, :])
+
+        with tc.manual_schedule():
+            load_x(0)
+            load_weight(0, Wq_words, Wq_scales)
+            load_x(1)
+            load_weight(1, Wk_words, Wk_scales)
+            load_table(SIN, sin2)
+            load_table(COS, cos2)
+            for c in range(2, AHEAD):
+                load_x(c)
+
+            quantise(0, transpose_and_group(0))
+            nc.vector.tensor_scalar_mul(
+                out=table[:, NEG_SIN * PLANE : (NEG_SIN + 1) * PLANE],
+                in0=table[:, SIN * PLANE : (SIN + 1) * PLANE],
+                scalar1=-1.0,
+            )
+            for c in range(1, CHUNKS):
+                grouped = transpose_and_group(c)
+                project(c - 1)
+                quantise(c, grouped)
+                rotate_and_store(c - 1)
+                if c - 1 + AHEAD < CHUNKS:
+                    load_x(c - 1 + AHEAD)
+            project(CHUNKS - 1)
+            rotate_and_store(CHUNKS - 1)

@@ -44,7 +44,7 @@ def tile_multiheadselfattention_pa_t_kernel(
         x_pool = stack.enter_context(tc.tile_pool(name="x", bufs=AHEAD))
         grouped_pool = stack.enter_context(tc.tile_pool(name="grouped", bufs=2))
         mx_pool = stack.enter_context(tc.tile_pool(name="mx", bufs=3))
-        product_pool = stack.enter_context(tc.tile_pool(name="product", bufs=4))
+        product_pool = stack.enter_context(tc.tile_pool(name="product", bufs=6))
         out_pool = stack.enter_context(tc.tile_pool(name="out", bufs=6))
         flipped_pool = stack.enter_context(tc.psum_pool(name="flipped", bufs=TILES))
         sums_pool = stack.enter_context(tc.psum_pool(name="sums", bufs=TILES))
@@ -175,7 +175,7 @@ def tile_multiheadselfattention_pa_t_kernel(
                 products.append((from_even, from_odd))
             for half in range(TILES // 2):
                 from_even, from_odd = products[half]
-                nc.vector.tensor_tensor(
+                nc.gpsimd.tensor_tensor(
                     out=rotated[:, :, 2 * half : 2 * half + 2, :].rearrange("p w i d -> p w (i d)"),
                     in0=from_even[:].rearrange("p w n e -> p w (n e)"),
                     in1=from_odd[:].rearrange("p w n e -> p w (n e)"),

@@ -44,7 +44,7 @@ def tile_multiheadselfattention_pa_t_kernel(
         x_pool = stack.enter_context(tc.tile_pool(name="x", bufs=AHEAD))
         grouped_pool = stack.enter_context(tc.tile_pool(name="grouped", bufs=2))
         mx_pool = stack.enter_context(tc.tile_pool(name="mx", bufs=3))
-        product_pool = stack.enter_context(tc.tile_pool(name="product", bufs=6))
+        product_pool = stack.enter_context(tc.tile_pool(name="product", bufs=3))
         out_pool = stack.enter_context(tc.tile_pool(name="out", bufs=6))
         flipped_pool = stack.enter_context(tc.psum_pool(name="flipped", bufs=TILES))
         sums_pool = stack.enter_context(tc.psum_pool(name="sums", bufs=TILES))
@@ -154,33 +154,29 @@ def tile_multiheadselfattention_pa_t_kernel(
         def rotate_and_store(c):
             b, row0 = place(c)
             rotated = out_pool.tile([P, 2, TILES, HEAD], F32)
-            products = []
+            from_even = product_pool.tile([P, TILES // 2] + bank_shape[1:], F32)
+            from_odd = product_pool.tile([P, TILES // 2] + bank_shape[1:], F32)
             for half in range(TILES // 2):
                 pairs = sums_of[c][half][:].rearrange("p (w n e) -> p w n e", w=2, e=2)
                 row = row0 + 2 * half
-                from_even = product_pool.tile(bank_shape, F32)
                 nc.vector.tensor_tensor(
-                    out=from_even[:],
+                    out=from_even[:, half, :, :, :],
                     in0=pairs[:, :, :, 0:1].to_broadcast(bank_shape),
                     in1=factors(COS, row),
                     op=MULT,
                 )
-                from_odd = product_pool.tile(bank_shape, F32)
                 nc.vector.tensor_tensor(
-                    out=from_odd[:],
+                    out=from_odd[:, half, :, :, :],
                     in0=pairs[:, :, :, 1:2].to_broadcast(bank_shape),
                     in1=factors(NEG_SIN, row),
                     op=MULT,
                 )
-                products.append((from_even, from_odd))
-            for half in range(TILES // 2):
-                from_even, from_odd = products[half]
-                nc.gpsimd.tensor_tensor(
-                    out=rotated[:, :, 2 * half : 2 * half + 2, :].rearrange("p w i d -> p w (i d)"),
-                    in0=from_even[:].rearrange("p w n e -> p w (n e)"),
-                    in1=from_odd[:].rearrange("p w n e -> p w (n e)"),
-                    op=ADD,
-                )
+            nc.gpsimd.tensor_tensor(
+                out=rotated[:].rearrange("p w (h i) d -> p h w (i d)", h=TILES // 2),
+                in0=from_even[:].rearrange("p h w n e -> p h w (n e)"),
+                in1=from_odd[:].rearrange("p h w n e -> p h w (n e)"),
+                op=ADD,
+            )
             for w in range(2):
                 rows = outs[w][b, 0].rearrange("(p t) d -> p t d", t=ROWS)
                 nc.sync.dma_start(out=rows[:, row0 : row0 + TILES, :], in_=rotated[:, w, :, :])

@@ -22,15 +22,28 @@ K_PASS = 4 * P
 PASSES = D_MODEL // K_PASS
 ROWS = SEQ // P
 TILES = 4
-CHUNKS = BATCH * ROWS // TILES
-AHEAD = 8
-PLANE = ROWS * HEAD
+FIRST_SIZES = [1, 1, 2]
+AHEAD = 10
 NEG_SIN = 0
 COS = 1
 SIN = 2
 BANK = 512
+EARLY_ROWS = TILES
 
 FLOPS = 2 * BATCH * SEQ * D_MODEL * 2 * HEAD
+
+
+def chunk_list():
+    chunks = []
+    for b in range(BATCH):
+        sizes = [TILES] * (ROWS // TILES)
+        if b == 0:
+            sizes = FIRST_SIZES + sizes[1:]
+        row = 0
+        for size in sizes:
+            chunks.append((b, row, size))
+            row += size
+    return chunks
 
 
 def tile_multiheadselfattention_pa_t_kernel(
@@ -38,6 +51,7 @@ def tile_multiheadselfattention_pa_t_kernel(
 ):
     nc = tc.nc
     outs = [out_0, out_1]
+    chunks = chunk_list()
 
     with ExitStack() as stack:
         const = stack.enter_context(tc.tile_pool(name="const", bufs=1))
@@ -56,22 +70,24 @@ def tile_multiheadselfattention_pa_t_kernel(
         w_planes = const.tile([P, 2, PASSES, HEAD], U8, align_bytes=64)
         nc.vector.memset(w_planes[:].rearrange("p w g n -> p (w g n)").bitcast(I32), 0)
 
-        table = const.tile([P, 4 * PLANE], BF16)
+        early_table = const.tile([P, 4 * EARLY_ROWS * HEAD], BF16)
+        late_table = const.tile([P, 4 * (ROWS - EARLY_ROWS) * HEAD], BF16)
+
+        def table_of(row):
+            if row < EARLY_ROWS:
+                return early_table, row, EARLY_ROWS * HEAD
+            return late_table, row - EARLY_ROWS, (ROWS - EARLY_ROWS) * HEAD
 
         x_tiles = {}
         codes_of = {}
         planes_of = {}
         sums_of = {}
 
-        def place(c):
-            per_batch = ROWS // TILES
-            return c // per_batch, (c % per_batch) * TILES
-
         def load_x(c):
-            b, row0 = place(c)
+            b, row0, size = chunks[c]
             x_sb = x_pool.tile([P, TILES, D_MODEL], BF16)
             rows = x[b].rearrange("(p t) k -> p t k", t=ROWS)
-            nc.sync.dma_start(out=x_sb[:], in_=rows[:, row0 : row0 + TILES, :])
+            nc.sync.dma_start(out=x_sb[:, 0:size, :], in_=rows[:, row0 : row0 + size, :])
             x_tiles[c] = x_sb
 
         def load_weight(w, words, scales):
@@ -87,16 +103,28 @@ def tile_multiheadselfattention_pa_t_kernel(
                     ),
                 )
 
-        def load_table(plane, values):
+        def load_table(which, values, first_row, end_row):
+            table, place, plane = table_of(first_row)
             nc.sync.dma_start(
-                out=table[:, plane * PLANE : (plane + 1) * PLANE],
-                in_=values.rearrange("(p t) d -> p (t d)", t=ROWS),
+                out=table[:, which * plane : (which + 1) * plane],
+                in_=values.rearrange("(p t) d -> p t d", t=ROWS)[:, first_row:end_row, :].rearrange(
+                    "p t d -> p (t d)"
+                ),
+            )
+
+        def negate_sines(first_row):
+            table, place, plane = table_of(first_row)
+            nc.vector.tensor_scalar_mul(
+                out=table[:, NEG_SIN * plane : (NEG_SIN + 1) * plane],
+                in0=table[:, SIN * plane : (SIN + 1) * plane],
+                scalar1=-1.0,
             )
 
         def transpose_and_group(c):
+            size = chunks[c][2]
             grouped = grouped_pool.tile([P, TILES * D_MODEL], BF16, align_bytes=64)
             grouped_words = grouped[:].bitcast(F32)
-            for i in range(TILES):
+            for i in range(size):
                 words = x_tiles[c][:, i, :].bitcast(F32)
                 flipped = flipped_pool.tile([P, BANK], F32)
                 for g in range(PASSES):
@@ -115,25 +143,34 @@ def tile_multiheadselfattention_pa_t_kernel(
             return grouped
 
         def quantise(c, grouped):
+            size = chunks[c][2]
             codes = mx_pool.tile([P, TILES * PASSES * P], U32, align_bytes=64)
             planes = mx_pool.tile([P, TILES * PASSES * P], U8, align_bytes=64)
-            nc.vector.quantize_mx(out=codes[:].bitcast(FP8X4), scales=planes[:], in_=grouped[:])
+            nc.vector.quantize_mx(
+                out=codes[:, 0 : size * PASSES * P].bitcast(FP8X4),
+                scales=planes[:, 0 : size * PASSES * P],
+                in_=grouped[:, 0 : size * D_MODEL],
+            )
             codes_of[c] = codes
             planes_of[c] = planes
 
+        def per_bank(c):
+            return min(2, chunks[c][2])
+
         def project(c):
+            together = per_bank(c)
             sums_of[c] = []
-            for half in range(TILES // 2):
+            for bank in range(chunks[c][2] // together):
                 sums = sums_pool.tile([P, BANK], F32)
                 for w in range(2):
-                    for i in range(2):
+                    for i in range(together):
                         for g in range(PASSES):
                             tokens = slice(
-                                ((2 * half + i) * PASSES + g) * P,
-                                ((2 * half + i) * PASSES + g + 1) * P,
+                                ((together * bank + i) * PASSES + g) * P,
+                                ((together * bank + i) * PASSES + g + 1) * P,
                             )
                             nc.tensor.matmul_mx(
-                                out=sums[:, (2 * w + i) * HEAD : (2 * w + i + 1) * HEAD],
+                                out=sums[:, (together * w + i) * HEAD : (together * w + i + 1) * HEAD],
                                 lhsT=codes_of[c][:, tokens].bitcast(FP8X4),
                                 lhsT_scale=planes_of[c][:, tokens],
                                 rhs=w_words[:, w, g, :].bitcast(FP4X4),
@@ -143,66 +180,82 @@ def tile_multiheadselfattention_pa_t_kernel(
                             )
                 sums_of[c].append(sums)
 
-        bank_shape = [P, 2, HEAD, 2]
-
-        def factors(first, row):
-            start = first * PLANE + row * HEAD
-            window = table[:, start : start + 2 * (PLANE + 1)].rearrange("p (e n) -> p e n", e=2)
-            both = window[:, :, 0 : 2 * HEAD : 2].rearrange("p e n -> p n e")
-            return both.unsqueeze(1).to_broadcast(bank_shape)
+        def factors(first, row, shape):
+            table, place, plane = table_of(row)
+            start = first * plane + place * HEAD
+            window = table[:, start : start + 2 * (plane + 1)].rearrange("p (e n) -> p e n", e=2)
+            both = window[:, :, 0 : 2 * shape[2] : 2].rearrange("p e n -> p n e")
+            return both.unsqueeze(1).to_broadcast(shape)
 
         def rotate_and_store(c):
-            b, row0 = place(c)
+            b, row0, size = chunks[c]
+            together = per_bank(c)
+            width = 2 * together * HEAD
+            shape = [P, 2, width // 4, 2]
             rotated = out_pool.tile([P, 2, TILES, HEAD], F32)
-            from_even = product_pool.tile([P, TILES // 2] + bank_shape[1:], F32)
-            from_odd = product_pool.tile([P, TILES // 2] + bank_shape[1:], F32)
-            for half in range(TILES // 2):
-                pairs = sums_of[c][half][:].rearrange("p (w n e) -> p w n e", w=2, e=2)
-                row = row0 + 2 * half
+            from_even = product_pool.tile([P, 2 * TILES * HEAD], F32)
+            from_odd = product_pool.tile([P, 2 * TILES * HEAD], F32)
+            for bank in range(size // together):
+                pairs = sums_of[c][bank][:, 0:width].rearrange("p (w n e) -> p w n e", w=2, e=2)
+                row = row0 + together * bank
+                columns = slice(bank * width, (bank + 1) * width)
                 nc.vector.tensor_tensor(
-                    out=from_even[:, half, :, :, :],
-                    in0=pairs[:, :, :, 0:1].to_broadcast(bank_shape),
-                    in1=factors(COS, row),
+                    out=from_even[:, columns].rearrange("p (w n e) -> p w n e", w=2, e=2),
+                    in0=pairs[:, :, :, 0:1].to_broadcast(shape),
+                    in1=factors(COS, row, shape),
                     op=MULT,
                 )
                 nc.vector.tensor_tensor(
-                    out=from_odd[:, half, :, :, :],
-                    in0=pairs[:, :, :, 1:2].to_broadcast(bank_shape),
-                    in1=factors(NEG_SIN, row),
+                    out=from_odd[:, columns].rearrange("p (w n e) -> p w n e", w=2, e=2),
+                    in0=pairs[:, :, :, 1:2].to_broadcast(shape),
+                    in1=factors(NEG_SIN, row, shape),
                     op=MULT,
                 )
-            nc.gpsimd.tensor_tensor(
-                out=rotated[:].rearrange("p w (h i) d -> p h w (i d)", h=TILES // 2),
-                in0=from_even[:].rearrange("p h w n e -> p h w (n e)"),
-                in1=from_odd[:].rearrange("p h w n e -> p h w (n e)"),
-                op=ADD,
-            )
-            for w in range(2):
-                rows = outs[w][b, 0].rearrange("(p t) d -> p t d", t=ROWS)
-                nc.sync.dma_start(out=rows[:, row0 : row0 + TILES, :], in_=rotated[:, w, :, :])
+            banks = size // together
+            last = c == len(chunks) - 1
+            for first_bank, end_bank in [(h, h + 1) for h in range(banks)] if last else [(0, banks)]:
+                engine = nc.vector if last else nc.gpsimd
+                tiles = slice(first_bank * together, end_bank * together)
+                columns = slice(first_bank * width, end_bank * width)
+                engine.tensor_tensor(
+                    out=rotated[:, :, tiles, :].rearrange("p w (h i) d -> p h w (i d)", i=together),
+                    in0=from_even[:, columns].rearrange("p (h w c) -> p h w c", w=2, c=width // 2),
+                    in1=from_odd[:, columns].rearrange("p (h w c) -> p h w c", w=2, c=width // 2),
+                    op=ADD,
+                )
+                for w in range(2):
+                    rows = outs[w][b, 0].rearrange("(p t) d -> p t d", t=ROWS)
+                    nc.sync.dma_start(
+                        out=rows[:, row0 + tiles.start : row0 + tiles.stop, :],
+                        in_=rotated[:, w, tiles, :],
+                    )
 
         with tc.manual_schedule():
             load_x(0)
             load_weight(0, Wq_words, Wq_scales)
             load_x(1)
             load_weight(1, Wk_words, Wk_scales)
-            load_table(SIN, sin2)
-            load_table(COS, cos2)
-            for c in range(2, AHEAD):
+            load_x(2)
+            load_table(SIN, sin2, 0, EARLY_ROWS)
+            load_table(COS, cos2, 0, EARLY_ROWS)
+            load_x(3)
+            load_x(4)
+            load_table(SIN, sin2, EARLY_ROWS, ROWS)
+            load_table(COS, cos2, EARLY_ROWS, ROWS)
+            for c in range(5, AHEAD):
                 load_x(c)
 
             quantise(0, transpose_and_group(0))
-            nc.vector.tensor_scalar_mul(
-                out=table[:, NEG_SIN * PLANE : (NEG_SIN + 1) * PLANE],
-                in0=table[:, SIN * PLANE : (SIN + 1) * PLANE],
-                scalar1=-1.0,
-            )
-            for c in range(1, CHUNKS):
+            for c in range(1, len(chunks)):
                 grouped = transpose_and_group(c)
                 project(c - 1)
                 quantise(c, grouped)
+                if c == 1:
+                    negate_sines(0)
+                if c == len(FIRST_SIZES) + 1:
+                    negate_sines(EARLY_ROWS)
                 rotate_and_store(c - 1)
-                if c - 1 + AHEAD < CHUNKS:
+                if c - 1 + AHEAD < len(chunks):
                     load_x(c - 1 + AHEAD)
-            project(CHUNKS - 1)
-            rotate_and_store(CHUNKS - 1)
+            project(len(chunks) - 1)
+            rotate_and_store(len(chunks) - 1)

@@ -214,7 +214,7 @@ def tile_multiheadselfattention_pa_t_kernel(
             banks = size // together
             last = c == len(chunks) - 1
             for first_bank, end_bank in [(h, h + 1) for h in range(banks)] if last else [(0, banks)]:
-                engine = nc.vector if last else nc.gpsimd
+                engine = nc.vector if last or c < len(FIRST_SIZES) else nc.gpsimd
                 tiles = slice(first_bank * together, end_bank * together)
                 columns = slice(first_bank * width, end_bank * width)
                 engine.tensor_tensor(

@@ -12,6 +12,7 @@ FP8X4 = mybir.dt.float8_e4m3fn_x4
 FP4X4 = mybir.dt.float4_e2m1fn_x4
 MULT = mybir.AluOpType.mult
 ADD = mybir.AluOpType.add
+COPY = mybir.ActivationFunctionType.Copy
 
 P = 128
 BATCH = 4
@@ -24,11 +25,14 @@ ROWS = SEQ // P
 TILES = 4
 FIRST_SIZES = [1, 1, 2]
 AHEAD = 10
-NEG_SIN = 0
-COS = 1
-SIN = 2
 BANK = 512
-EARLY_ROWS = TILES
+TABLE_ROWS = 4
+PLANE = TABLE_ROWS * HEAD
+COS = 0
+SIN = 1
+NEG_SIN = 2
+COS_AGAIN = 3
+SHIFT = 2
 
 FLOPS = 2 * BATCH * SEQ * D_MODEL * 2 * HEAD
 
@@ -52,6 +56,7 @@ def tile_multiheadselfattention_pa_t_kernel(
     nc = tc.nc
     outs = [out_0, out_1]
     chunks = chunk_list()
+    last = len(chunks) - 1
 
     with ExitStack() as stack:
         const = stack.enter_context(tc.tile_pool(name="const", bufs=1))
@@ -61,7 +66,7 @@ def tile_multiheadselfattention_pa_t_kernel(
         product_pool = stack.enter_context(tc.tile_pool(name="product", bufs=3))
         out_pool = stack.enter_context(tc.tile_pool(name="out", bufs=6))
         flipped_pool = stack.enter_context(tc.psum_pool(name="flipped", bufs=TILES))
-        sums_pool = stack.enter_context(tc.psum_pool(name="sums", bufs=TILES))
+        sums_pool = stack.enter_context(tc.psum_pool(name="sums", bufs=4))
 
         identity = const.tile([P, P], F32)
         make_identity(nc, identity[:])
@@ -70,25 +75,28 @@ def tile_multiheadselfattention_pa_t_kernel(
         w_planes = const.tile([P, 2, PASSES, HEAD], U8, align_bytes=64)
         nc.vector.memset(w_planes[:].rearrange("p w g n -> p (w g n)").bitcast(I32), 0)
 
-        early_table = const.tile([P, 4 * EARLY_ROWS * HEAD], BF16)
-        late_table = const.tile([P, 4 * (ROWS - EARLY_ROWS) * HEAD], BF16)
-
-        def table_of(row):
-            if row < EARLY_ROWS:
-                return early_table, row, EARLY_ROWS * HEAD
-            return late_table, row - EARLY_ROWS, (ROWS - EARLY_ROWS) * HEAD
+        pieces = []
+        for index in range(ROWS // TABLE_ROWS):
+            table = const.tile([P, 4 * (PLANE + 1)], BF16, name="table%d" % index)
+            pieces.append(table)
 
         x_tiles = {}
         codes_of = {}
         planes_of = {}
         sums_of = {}
+        products = {}
 
-        def load_x(c):
+        def load_x(c, first_tile=0, end_tile=None):
             b, row0, size = chunks[c]
-            x_sb = x_pool.tile([P, TILES, D_MODEL], BF16)
+            end_tile = end_tile or size
+            if c not in x_tiles:
+                x_sb = x_pool.tile([P, TILES, D_MODEL], BF16, name="x_sb")
+                x_tiles[c] = x_sb
             rows = x[b].rearrange("(p t) k -> p t k", t=ROWS)
-            nc.sync.dma_start(out=x_sb[:, 0:size, :], in_=rows[:, row0 : row0 + size, :])
-            x_tiles[c] = x_sb
+            nc.sync.dma_start(
+                out=x_tiles[c][:, first_tile:end_tile, :],
+                in_=rows[:, row0 + first_tile : row0 + end_tile, :],
+            )
 
         def load_weight(w, words, scales):
             nc.sync.dma_start(
@@ -103,21 +111,28 @@ def tile_multiheadselfattention_pa_t_kernel(
                     ),
                 )
 
-        def load_table(which, values, first_row, end_row):
-            table, place, plane = table_of(first_row)
-            nc.sync.dma_start(
-                out=table[:, which * plane : (which + 1) * plane],
-                in_=values.rearrange("(p t) d -> p t d", t=ROWS)[:, first_row:end_row, :].rearrange(
-                    "p t d -> p (t d)"
-                ),
-            )
+        def load_tables(index):
+            table = pieces[index]
+            first = TABLE_ROWS * index
+            for which, values in [(COS, cos2), (SIN, sin2)]:
+                nc.sync.dma_start(
+                    out=table[:, which * PLANE : (which + 1) * PLANE],
+                    in_=values.rearrange("(p t) d -> p t d", t=ROWS)[
+                        :, first : first + TABLE_ROWS, :
+                    ].rearrange("p t d -> p (t d)"),
+                )
 
-        def negate_sines(first_row):
-            table, place, plane = table_of(first_row)
-            nc.vector.tensor_scalar_mul(
-                out=table[:, NEG_SIN * plane : (NEG_SIN + 1) * plane],
-                in0=table[:, SIN * plane : (SIN + 1) * plane],
-                scalar1=-1.0,
+        def prepare_tables(index):
+            table = pieces[index]
+            nc.scalar.activation(
+                out=table[:, NEG_SIN * PLANE + SHIFT : (NEG_SIN + 1) * PLANE + SHIFT],
+                in_=table[:, SIN * PLANE : (SIN + 1) * PLANE],
+                func=COPY,
+                scale=-1.0,
+            )
+            nc.scalar.copy(
+                out=table[:, COS_AGAIN * PLANE + SHIFT : (COS_AGAIN + 1) * PLANE + SHIFT],
+                in_=table[:, COS * PLANE : (COS + 1) * PLANE],
             )
 
         def transpose_and_group(c):
@@ -154,108 +169,101 @@ def tile_multiheadselfattention_pa_t_kernel(
             codes_of[c] = codes
             planes_of[c] = planes
 
-        def per_bank(c):
-            return min(2, chunks[c][2])
-
         def project(c):
-            together = per_bank(c)
             sums_of[c] = []
-            for bank in range(chunks[c][2] // together):
+            for w in range(2):
                 sums = sums_pool.tile([P, BANK], F32)
-                for w in range(2):
-                    for i in range(together):
-                        for g in range(PASSES):
-                            tokens = slice(
-                                ((together * bank + i) * PASSES + g) * P,
-                                ((together * bank + i) * PASSES + g + 1) * P,
-                            )
-                            nc.tensor.matmul_mx(
-                                out=sums[:, (together * w + i) * HEAD : (together * w + i + 1) * HEAD],
-                                lhsT=codes_of[c][:, tokens].bitcast(FP8X4),
-                                lhsT_scale=planes_of[c][:, tokens],
-                                rhs=w_words[:, w, g, :].bitcast(FP4X4),
-                                rhs_scale=w_planes[:, w, g, :],
-                                start=(g == 0),
-                                stop=(g == PASSES - 1),
-                            )
+                for i in range(chunks[c][2]):
+                    for g in range(PASSES):
+                        tokens = slice((i * PASSES + g) * P, (i * PASSES + g + 1) * P)
+                        nc.tensor.matmul_mx(
+                            out=sums[:, i * HEAD : (i + 1) * HEAD],
+                            lhsT=codes_of[c][:, tokens].bitcast(FP8X4),
+                            lhsT_scale=planes_of[c][:, tokens],
+                            rhs=w_words[:, w, g, :].bitcast(FP4X4),
+                            rhs_scale=w_planes[:, w, g, :],
+                            start=(g == 0),
+                            stop=(g == PASSES - 1),
+                        )
                 sums_of[c].append(sums)
 
-        def factors(first, row, shape):
-            table, place, plane = table_of(row)
-            start = first * plane + place * HEAD
-            window = table[:, start : start + 2 * (plane + 1)].rearrange("p (e n) -> p e n", e=2)
-            both = window[:, :, 0 : 2 * shape[2] : 2].rearrange("p e n -> p n e")
-            return both.unsqueeze(1).to_broadcast(shape)
+        def factors(row, size):
+            place = row % TABLE_ROWS * HEAD
+            rows = pieces[row // TABLE_ROWS][:].rearrange("p (a e n) -> p a e n", a=2, e=2)
+            return rows[:, :, :, place : place + size * HEAD : 2].rearrange("p a e n -> p a n e")
+
+        def multiply(c, w):
+            b, row0, size = chunks[c]
+            width = size * HEAD
+            if w == 0:
+                product = product_pool.tile([P, 2, 2 * BANK], F32)
+                products[c] = product
+            sums = sums_of[c][w][:, 0:width].rearrange("p (n a) -> p a n", a=2)
+            nc.vector.tensor_tensor(
+                out=products[c][:, :, w * width : (w + 1) * width].rearrange(
+                    "p a (n e) -> p a n e", e=2
+                ),
+                in0=sums.unsqueeze(3).to_broadcast([P, 2, width // 2, 2]),
+                in1=factors(row0, size),
+                op=MULT,
+            )
+
+        def add_and_store(c, engine):
+            b, row0, size = chunks[c]
+            width = size * HEAD
+            rotated = out_pool.tile([P, 2 * BANK], F32)
+            engine.tensor_tensor(
+                out=rotated[:, 0 : 2 * width],
+                in0=products[c][:, 0, 0 : 2 * width],
+                in1=products[c][:, 1, 0 : 2 * width],
+                op=ADD,
+            )
+            for w in range(2):
+                nc.sync.dma_start(
+                    out=outs[w][b, 0].rearrange("(p t) d -> p t d", t=ROWS)[
+                        :, row0 : row0 + size, :
+                    ],
+                    in_=rotated[:, w * width : (w + 1) * width].rearrange(
+                        "p (t d) -> p t d", d=HEAD
+                    ),
+                )
 
         def rotate_and_store(c):
-            b, row0, size = chunks[c]
-            together = per_bank(c)
-            width = 2 * together * HEAD
-            shape = [P, 2, width // 4, 2]
-            rotated = out_pool.tile([P, 2, TILES, HEAD], F32)
-            from_even = product_pool.tile([P, 2 * TILES * HEAD], F32)
-            from_odd = product_pool.tile([P, 2 * TILES * HEAD], F32)
-            for bank in range(size // together):
-                pairs = sums_of[c][bank][:, 0:width].rearrange("p (w n e) -> p w n e", w=2, e=2)
-                row = row0 + together * bank
-                columns = slice(bank * width, (bank + 1) * width)
-                nc.vector.tensor_tensor(
-                    out=from_even[:, columns].rearrange("p (w n e) -> p w n e", w=2, e=2),
-                    in0=pairs[:, :, :, 0:1].to_broadcast(shape),
-                    in1=factors(COS, row, shape),
-                    op=MULT,
-                )
-                nc.vector.tensor_tensor(
-                    out=from_odd[:, columns].rearrange("p (w n e) -> p w n e", w=2, e=2),
-                    in0=pairs[:, :, :, 1:2].to_broadcast(shape),
-                    in1=factors(NEG_SIN, row, shape),
-                    op=MULT,
-                )
-            banks = size // together
-            last = c == len(chunks) - 1
-            for first_bank, end_bank in [(h, h + 1) for h in range(banks)] if last else [(0, banks)]:
-                engine = nc.vector if last or c < len(FIRST_SIZES) else nc.gpsimd
-                tiles = slice(first_bank * together, end_bank * together)
-                columns = slice(first_bank * width, end_bank * width)
-                engine.tensor_tensor(
-                    out=rotated[:, :, tiles, :].rearrange("p w (h i) d -> p h w (i d)", i=together),
-                    in0=from_even[:, columns].rearrange("p (h w c) -> p h w c", w=2, c=width // 2),
-                    in1=from_odd[:, columns].rearrange("p (h w c) -> p h w c", w=2, c=width // 2),
-                    op=ADD,
-                )
-                for w in range(2):
-                    rows = outs[w][b, 0].rearrange("(p t) d -> p t d", t=ROWS)
-                    nc.sync.dma_start(
-                        out=rows[:, row0 + tiles.start : row0 + tiles.stop, :],
-                        in_=rotated[:, w, tiles, :],
-                    )
+            multiply(c, 0)
+            multiply(c, 1)
+            on_vector = c < len(FIRST_SIZES) or c == last
+            add_and_store(c, nc.vector if on_vector else nc.gpsimd)
 
         with tc.manual_schedule():
             load_x(0)
             load_weight(0, Wq_words, Wq_scales)
             load_x(1)
             load_weight(1, Wk_words, Wk_scales)
+            load_tables(0)
             load_x(2)
-            load_table(SIN, sin2, 0, EARLY_ROWS)
-            load_table(COS, cos2, 0, EARLY_ROWS)
-            load_x(3)
-            load_x(4)
-            load_table(SIN, sin2, EARLY_ROWS, ROWS)
-            load_table(COS, cos2, EARLY_ROWS, ROWS)
-            for c in range(5, AHEAD):
+            load_x(3, 0, 2)
+            load_x(3, 2, 4)
+            load_tables(1)
+            load_x(4, 0, 2)
+            load_x(4, 2, 4)
+            load_x(5, 0, 2)
+            load_x(5, 2, 4)
+            load_tables(2)
+            load_x(6)
+            load_tables(3)
+            for c in range(7, AHEAD):
                 load_x(c)
 
+            table_at = {1: 0, 4: 1, 5: 2, 6: 3}
             quantise(0, transpose_and_group(0))
             for c in range(1, len(chunks)):
                 grouped = transpose_and_group(c)
                 project(c - 1)
                 quantise(c, grouped)
-                if c == 1:
-                    negate_sines(0)
-                if c == len(FIRST_SIZES) + 1:
-                    negate_sines(EARLY_ROWS)
+                if c in table_at:
+                    prepare_tables(table_at[c])
                 rotate_and_store(c - 1)
                 if c - 1 + AHEAD < len(chunks):
                     load_x(c - 1 + AHEAD)
-            project(len(chunks) - 1)
-            rotate_and_store(len(chunks) - 1)
+            project(last)
+            rotate_and_store(last)

@@ -26,6 +26,8 @@ TILES = 4
 FIRST_SIZES = [1, 1, 2]
 AHEAD = 10
 BANK = 512
+STRIP = 160
+LAP = 8
 TABLE_ROWS = 4
 PLANE = TABLE_ROWS * HEAD
 COS = 0
@@ -124,16 +126,16 @@ def tile_multiheadselfattention_pa_t_kernel(
 
         def prepare_tables(index):
             table = pieces[index]
-            nc.scalar.activation(
-                out=table[:, NEG_SIN * PLANE + SHIFT : (NEG_SIN + 1) * PLANE + SHIFT],
-                in_=table[:, SIN * PLANE : (SIN + 1) * PLANE],
-                func=COPY,
-                scale=-1.0,
-            )
-            nc.scalar.copy(
-                out=table[:, COS_AGAIN * PLANE + SHIFT : (COS_AGAIN + 1) * PLANE + SHIFT],
-                in_=table[:, COS * PLANE : (COS + 1) * PLANE],
-            )
+            negated = table[:, NEG_SIN * PLANE + SHIFT : (NEG_SIN + 1) * PLANE + SHIFT]
+            again = table[:, COS_AGAIN * PLANE + SHIFT : (COS_AGAIN + 1) * PLANE + SHIFT]
+            sines = table[:, SIN * PLANE : (SIN + 1) * PLANE]
+            cosines = table[:, COS * PLANE : (COS + 1) * PLANE]
+            if index == 0:
+                nc.vector.tensor_scalar_mul(out=negated, in0=sines, scalar1=-1.0)
+                nc.vector.tensor_copy(out=again, in_=cosines)
+            else:
+                nc.scalar.activation(out=negated, in_=sines, func=COPY, scale=-1.0)
+                nc.scalar.copy(out=again, in_=cosines)
 
         def transpose_and_group(c):
             size = chunks[c][2]
@@ -208,16 +210,25 @@ def tile_multiheadselfattention_pa_t_kernel(
                 op=MULT,
             )
 
-        def add_and_store(c, engine):
-            b, row0, size = chunks[c]
-            width = size * HEAD
-            rotated = out_pool.tile([P, 2 * BANK], F32)
+        def add(engine, c, rotated, first, end):
             engine.tensor_tensor(
-                out=rotated[:, 0 : 2 * width],
-                in0=products[c][:, 0, 0 : 2 * width],
-                in1=products[c][:, 1, 0 : 2 * width],
+                out=rotated[:, first:end],
+                in0=products[c][:, 0, first:end],
+                in1=products[c][:, 1, first:end],
                 op=ADD,
             )
+
+        def rotate_and_store(c):
+            b, row0, size = chunks[c]
+            width = size * HEAD
+            multiply(c, 0)
+            multiply(c, 1)
+            rotated = out_pool.tile([P, 2 * BANK], F32)
+            if c < len(FIRST_SIZES) or c == last:
+                add(nc.vector, c, rotated, 0, 2 * width)
+            else:
+                add(nc.vector, c, rotated, 0, STRIP)
+                add(nc.gpsimd, c, rotated, STRIP - LAP, 2 * width)
             for w in range(2):
                 nc.sync.dma_start(
                     out=outs[w][b, 0].rearrange("(p t) d -> p t d", t=ROWS)[
@@ -228,24 +239,18 @@ def tile_multiheadselfattention_pa_t_kernel(
                     ),
                 )
 
-        def rotate_and_store(c):
-            multiply(c, 0)
-            multiply(c, 1)
-            on_vector = c < len(FIRST_SIZES) or c == last
-            add_and_store(c, nc.vector if on_vector else nc.gpsimd)
-
         with tc.manual_schedule():
             load_x(0)
             load_weight(0, Wq_words, Wq_scales)
             load_x(1)
             load_weight(1, Wk_words, Wk_scales)
-            load_tables(0)
             load_x(2)
+            load_tables(0)
             load_x(3, 0, 2)
             load_x(3, 2, 4)
-            load_tables(1)
             load_x(4, 0, 2)
             load_x(4, 2, 4)
+            load_tables(1)
             load_x(5, 0, 2)
             load_x(5, 2, 4)
             load_tables(2)

@@ -25,16 +25,13 @@ ROWS = SEQ // P
 TILES = 4
 FIRST_SIZES = [1, 1, 2]
 AHEAD = 10
+FIRST_SORTED = len(FIRST_SIZES) + 2
 BANK = 512
-STRIP = 160
-LAP = 8
 TABLE_ROWS = 4
 PLANE = TABLE_ROWS * HEAD
-COS = 0
-SIN = 1
-NEG_SIN = 2
-COS_AGAIN = 3
-SHIFT = 2
+NEG_SIN = 0
+COS = 1
+SIN = 2
 
 FLOPS = 2 * BATCH * SEQ * D_MODEL * 2 * HEAD
 
@@ -67,6 +64,7 @@ def tile_multiheadselfattention_pa_t_kernel(
         mx_pool = stack.enter_context(tc.tile_pool(name="mx", bufs=3))
         product_pool = stack.enter_context(tc.tile_pool(name="product", bufs=3))
         out_pool = stack.enter_context(tc.tile_pool(name="out", bufs=6))
+        sorted_pool = stack.enter_context(tc.tile_pool(name="sorted", bufs=3))
         flipped_pool = stack.enter_context(tc.psum_pool(name="flipped", bufs=TILES))
         sums_pool = stack.enter_context(tc.psum_pool(name="sums", bufs=4))
 
@@ -79,7 +77,7 @@ def tile_multiheadselfattention_pa_t_kernel(
 
         pieces = []
         for index in range(ROWS // TABLE_ROWS):
-            table = const.tile([P, 4 * (PLANE + 1)], BF16, name="table%d" % index)
+            table = const.tile([P, 4 * PLANE], BF16, name="table%d" % index)
             pieces.append(table)
 
         x_tiles = {}
@@ -87,6 +85,7 @@ def tile_multiheadselfattention_pa_t_kernel(
         planes_of = {}
         sums_of = {}
         products = {}
+        sorted_tiles = {}
 
         def load_x(c, first_tile=0, end_tile=None):
             b, row0, size = chunks[c]
@@ -124,18 +123,24 @@ def tile_multiheadselfattention_pa_t_kernel(
                     ].rearrange("p t d -> p (t d)"),
                 )
 
-        def prepare_tables(index):
+        def negate_sines(index):
             table = pieces[index]
-            negated = table[:, NEG_SIN * PLANE + SHIFT : (NEG_SIN + 1) * PLANE + SHIFT]
-            again = table[:, COS_AGAIN * PLANE + SHIFT : (COS_AGAIN + 1) * PLANE + SHIFT]
+            negated = table[:, NEG_SIN * PLANE : (NEG_SIN + 1) * PLANE]
             sines = table[:, SIN * PLANE : (SIN + 1) * PLANE]
-            cosines = table[:, COS * PLANE : (COS + 1) * PLANE]
             if index == 0:
                 nc.vector.tensor_scalar_mul(out=negated, in0=sines, scalar1=-1.0)
-                nc.vector.tensor_copy(out=again, in_=cosines)
             else:
                 nc.scalar.activation(out=negated, in_=sines, func=COPY, scale=-1.0)
-                nc.scalar.copy(out=again, in_=cosines)
+
+        def sort_words(c):
+            words = sorted_pool.tile([P, BANK], F32)
+            nc.scalar.copy(
+                out=words[:].rearrange("p (g u n) -> p g u n", g=PASSES, u=2),
+                in_=x_tiles[c][:, TILES - 1, :]
+                .bitcast(F32)
+                .rearrange("p (g n u) -> p g u n", g=PASSES, u=2),
+            )
+            sorted_tiles[c] = words
 
         def transpose_and_group(c):
             size = chunks[c][2]
@@ -143,12 +148,15 @@ def tile_multiheadselfattention_pa_t_kernel(
             grouped_words = grouped[:].bitcast(F32)
             for i in range(size):
                 words = x_tiles[c][:, i, :].bitcast(F32)
+                is_sorted = i == TILES - 1 and c in sorted_tiles
                 flipped = flipped_pool.tile([P, BANK], F32)
                 for g in range(PASSES):
                     for u in range(2):
+                        place = slice((2 * g + u) * P, (2 * g + u + 1) * P)
+                        every_second = words[:, 2 * P * g + u : 2 * P * (g + 1) : 2]
                         nc.tensor.transpose(
-                            flipped[:, (2 * g + u) * P : (2 * g + u + 1) * P],
-                            words[:, 2 * P * g + u : 2 * P * (g + 1) : 2],
+                            flipped[:, place],
+                            sorted_tiles[c][:, place] if is_sorted else every_second,
                             identity[:],
                         )
                 nc.scalar.copy(
@@ -189,10 +197,11 @@ def tile_multiheadselfattention_pa_t_kernel(
                         )
                 sums_of[c].append(sums)
 
-        def factors(row, size):
-            place = row % TABLE_ROWS * HEAD
-            rows = pieces[row // TABLE_ROWS][:].rearrange("p (a e n) -> p a e n", a=2, e=2)
-            return rows[:, :, :, place : place + size * HEAD : 2].rearrange("p a e n -> p a n e")
+        def factors(first, row, size):
+            start = first * PLANE + row % TABLE_ROWS * HEAD
+            window = pieces[row // TABLE_ROWS][:, start : start + 2 * (PLANE + 1)]
+            rows = window.rearrange("p (e n) -> p e n", e=2)
+            return rows[:, :, 0 : size * HEAD : 2].rearrange("p e n -> p n e")
 
         def multiply(c, w):
             b, row0, size = chunks[c]
@@ -200,21 +209,22 @@ def tile_multiheadselfattention_pa_t_kernel(
             if w == 0:
                 product = product_pool.tile([P, 2, 2 * BANK], F32)
                 products[c] = product
-            sums = sums_of[c][w][:, 0:width].rearrange("p (n a) -> p a n", a=2)
-            nc.vector.tensor_tensor(
-                out=products[c][:, :, w * width : (w + 1) * width].rearrange(
-                    "p a (n e) -> p a n e", e=2
-                ),
-                in0=sums.unsqueeze(3).to_broadcast([P, 2, width // 2, 2]),
-                in1=factors(row0, size),
-                op=MULT,
-            )
+            pairs = sums_of[c][w][:, 0:width].rearrange("p (n a) -> p n a", a=2)
+            for a, first_table in enumerate([COS, NEG_SIN]):
+                nc.vector.tensor_tensor(
+                    out=products[c][:, a, w * width : (w + 1) * width].rearrange(
+                        "p (n e) -> p n e", e=2
+                    ),
+                    in0=pairs[:, :, a : a + 1].to_broadcast([P, width // 2, 2]),
+                    in1=factors(first_table, row0, size),
+                    op=MULT,
+                )
 
-        def add(engine, c, rotated, first, end):
+        def add(engine, c, rotated, end):
             engine.tensor_tensor(
-                out=rotated[:, first:end],
-                in0=products[c][:, 0, first:end],
-                in1=products[c][:, 1, first:end],
+                out=rotated[:, 0:end],
+                in0=products[c][:, 0, 0:end],
+                in1=products[c][:, 1, 0:end],
                 op=ADD,
             )
 
@@ -224,11 +234,7 @@ def tile_multiheadselfattention_pa_t_kernel(
             multiply(c, 0)
             multiply(c, 1)
             rotated = out_pool.tile([P, 2 * BANK], F32)
-            if c < len(FIRST_SIZES) or c == last:
-                add(nc.vector, c, rotated, 0, 2 * width)
-            else:
-                add(nc.vector, c, rotated, 0, STRIP)
-                add(nc.gpsimd, c, rotated, STRIP - LAP, 2 * width)
+            add(nc.vector if c < len(FIRST_SIZES) or c == last else nc.gpsimd, c, rotated, 2 * width)
             for w in range(2):
                 nc.sync.dma_start(
                     out=outs[w][b, 0].rearrange("(p t) d -> p t d", t=ROWS)[
@@ -243,10 +249,10 @@ def tile_multiheadselfattention_pa_t_kernel(
             load_x(0)
             load_weight(0, Wq_words, Wq_scales)
             load_x(1)
-            load_weight(1, Wk_words, Wk_scales)
             load_x(2)
-            load_tables(0)
+            load_weight(1, Wk_words, Wk_scales)
             load_x(3, 0, 2)
+            load_tables(0)
             load_x(3, 2, 4)
             load_x(4, 0, 2)
             load_x(4, 2, 4)
@@ -263,10 +269,12 @@ def tile_multiheadselfattention_pa_t_kernel(
             quantise(0, transpose_and_group(0))
             for c in range(1, len(chunks)):
                 grouped = transpose_and_group(c)
+                if FIRST_SORTED <= c + 1 < len(chunks):
+                    sort_words(c + 1)
                 project(c - 1)
                 quantise(c, grouped)
                 if c in table_at:
-                    prepare_tables(table_at[c])
+                    negate_sines(table_at[c])
                 rotate_and_store(c - 1)
                 if c - 1 + AHEAD < len(chunks):
                     load_x(c - 1 + AHEAD)

@@ -25,7 +25,8 @@ ROWS = SEQ // P
 TILES = 4
 FIRST_SIZES = [1, 1, 2]
 AHEAD = 10
-FIRST_SORTED = len(FIRST_SIZES) + 2
+ON_VECTOR = 2
+TOKEN = 8
 BANK = 512
 TABLE_ROWS = 4
 PLANE = TABLE_ROWS * HEAD
@@ -64,7 +65,6 @@ def tile_multiheadselfattention_pa_t_kernel(
         mx_pool = stack.enter_context(tc.tile_pool(name="mx", bufs=3))
         product_pool = stack.enter_context(tc.tile_pool(name="product", bufs=3))
         out_pool = stack.enter_context(tc.tile_pool(name="out", bufs=6))
-        sorted_pool = stack.enter_context(tc.tile_pool(name="sorted", bufs=3))
         flipped_pool = stack.enter_context(tc.psum_pool(name="flipped", bufs=TILES))
         sums_pool = stack.enter_context(tc.psum_pool(name="sums", bufs=4))
 
@@ -85,7 +85,7 @@ def tile_multiheadselfattention_pa_t_kernel(
         planes_of = {}
         sums_of = {}
         products = {}
-        sorted_tiles = {}
+        rotated_of = {}
 
         def load_x(c, first_tile=0, end_tile=None):
             b, row0, size = chunks[c]
@@ -132,31 +132,18 @@ def tile_multiheadselfattention_pa_t_kernel(
             else:
                 nc.scalar.activation(out=negated, in_=sines, func=COPY, scale=-1.0)
 
-        def sort_words(c):
-            words = sorted_pool.tile([P, BANK], F32)
-            nc.scalar.copy(
-                out=words[:].rearrange("p (g u n) -> p g u n", g=PASSES, u=2),
-                in_=x_tiles[c][:, TILES - 1, :]
-                .bitcast(F32)
-                .rearrange("p (g n u) -> p g u n", g=PASSES, u=2),
-            )
-            sorted_tiles[c] = words
-
         def transpose_and_group(c):
             size = chunks[c][2]
             grouped = grouped_pool.tile([P, TILES * D_MODEL], BF16, align_bytes=64)
             grouped_words = grouped[:].bitcast(F32)
             for i in range(size):
                 words = x_tiles[c][:, i, :].bitcast(F32)
-                is_sorted = i == TILES - 1 and c in sorted_tiles
                 flipped = flipped_pool.tile([P, BANK], F32)
                 for g in range(PASSES):
                     for u in range(2):
-                        place = slice((2 * g + u) * P, (2 * g + u + 1) * P)
-                        every_second = words[:, 2 * P * g + u : 2 * P * (g + 1) : 2]
                         nc.tensor.transpose(
-                            flipped[:, place],
-                            sorted_tiles[c][:, place] if is_sorted else every_second,
+                            flipped[:, (2 * g + u) * P : (2 * g + u + 1) * P],
+                            words[:, 2 * P * g + u : 2 * P * (g + 1) : 2],
                             identity[:],
                         )
                 nc.scalar.copy(
@@ -220,21 +207,23 @@ def tile_multiheadselfattention_pa_t_kernel(
                     op=MULT,
                 )
 
-        def add(engine, c, rotated, end):
-            engine.tensor_tensor(
-                out=rotated[:, 0:end],
-                in0=products[c][:, 0, 0:end],
-                in1=products[c][:, 1, 0:end],
-                op=ADD,
-            )
+        def new_output(c):
+            rotated = out_pool.tile([P, 2 * BANK], F32, name="rotated")
+            rotated_of[c] = rotated
 
-        def rotate_and_store(c):
+        def mark_output(c):
+            nc.scalar.copy(out=rotated_of[c][:, 0:TOKEN], in_=identity[:, 0:TOKEN])
+
+        def add_and_store(c, engine):
             b, row0, size = chunks[c]
             width = size * HEAD
-            multiply(c, 0)
-            multiply(c, 1)
-            rotated = out_pool.tile([P, 2 * BANK], F32)
-            add(nc.vector if c < len(FIRST_SIZES) or c == last else nc.gpsimd, c, rotated, 2 * width)
+            rotated = rotated_of[c]
+            engine.tensor_tensor(
+                out=rotated[:, 0 : 2 * width],
+                in0=products[c][:, 0, 0 : 2 * width],
+                in1=products[c][:, 1, 0 : 2 * width],
+                op=ADD,
+            )
             for w in range(2):
                 nc.sync.dma_start(
                     out=outs[w][b, 0].rearrange("(p t) d -> p t d", t=ROWS)[
@@ -244,6 +233,13 @@ def tile_multiheadselfattention_pa_t_kernel(
                         "p (t d) -> p t d", d=HEAD
                     ),
                 )
+
+        def rotate(c):
+            multiply(c, 0)
+            multiply(c, 1)
+            new_output(c)
+            if c < ON_VECTOR or c == last:
+                add_and_store(c, nc.vector)
 
         with tc.manual_schedule():
             load_x(0)
@@ -269,14 +265,17 @@ def tile_multiheadselfattention_pa_t_kernel(
             quantise(0, transpose_and_group(0))
             for c in range(1, len(chunks)):
                 grouped = transpose_and_group(c)
-                if FIRST_SORTED <= c + 1 < len(chunks):
-                    sort_words(c + 1)
+                if c - 2 >= ON_VECTOR:
+                    mark_output(c - 2)
                 project(c - 1)
                 quantise(c, grouped)
                 if c in table_at:
                     negate_sines(table_at[c])
-                rotate_and_store(c - 1)
+                if c - 2 >= ON_VECTOR:
+                    add_and_store(c - 2, nc.gpsimd)
+                rotate(c - 1)
                 if c - 1 + AHEAD < len(chunks):
                     load_x(c - 1 + AHEAD)
             project(last)
-            rotate_and_store(last)
+            add_and_store(last - 1, nc.gpsimd)
+            rotate(last)

@@ -30,9 +30,11 @@ TOKEN = 8
 BANK = 512
 TABLE_ROWS = 4
 PLANE = TABLE_ROWS * HEAD
-NEG_SIN = 0
-COS = 1
-SIN = 2
+COS = 0
+SIN = 1
+NEG_SIN = 2
+COS_AGAIN = 3
+SHIFT = 2
 
 FLOPS = 2 * BATCH * SEQ * D_MODEL * 2 * HEAD
 
@@ -77,7 +79,7 @@ def tile_multiheadselfattention_pa_t_kernel(
 
         pieces = []
         for index in range(ROWS // TABLE_ROWS):
-            table = const.tile([P, 4 * PLANE], BF16, name="table%d" % index)
+            table = const.tile([P, 4 * (PLANE + 1)], BF16, name="table%d" % index)
             pieces.append(table)
 
         x_tiles = {}
@@ -123,14 +125,18 @@ def tile_multiheadselfattention_pa_t_kernel(
                     ].rearrange("p t d -> p (t d)"),
                 )
 
-        def negate_sines(index):
+        def prepare_tables(index):
             table = pieces[index]
-            negated = table[:, NEG_SIN * PLANE : (NEG_SIN + 1) * PLANE]
+            negated = table[:, NEG_SIN * PLANE + SHIFT : (NEG_SIN + 1) * PLANE + SHIFT]
+            again = table[:, COS_AGAIN * PLANE + SHIFT : (COS_AGAIN + 1) * PLANE + SHIFT]
             sines = table[:, SIN * PLANE : (SIN + 1) * PLANE]
+            cosines = table[:, COS * PLANE : (COS + 1) * PLANE]
             if index == 0:
                 nc.vector.tensor_scalar_mul(out=negated, in0=sines, scalar1=-1.0)
+                nc.vector.tensor_copy(out=again, in_=cosines)
             else:
                 nc.scalar.activation(out=negated, in_=sines, func=COPY, scale=-1.0)
+                nc.scalar.copy(out=again, in_=cosines)
 
         def transpose_and_group(c):
             size = chunks[c][2]
@@ -184,11 +190,10 @@ def tile_multiheadselfattention_pa_t_kernel(
                         )
                 sums_of[c].append(sums)
 
-        def factors(first, row, size):
-            start = first * PLANE + row % TABLE_ROWS * HEAD
-            window = pieces[row // TABLE_ROWS][:, start : start + 2 * (PLANE + 1)]
-            rows = window.rearrange("p (e n) -> p e n", e=2)
-            return rows[:, :, 0 : size * HEAD : 2].rearrange("p e n -> p n e")
+        def factors(row, size):
+            place = row % TABLE_ROWS * HEAD
+            rows = pieces[row // TABLE_ROWS][:].rearrange("p (a e n) -> p a e n", a=2, e=2)
+            return rows[:, :, :, place : place + size * HEAD : 2].rearrange("p a e n -> p a n e")
 
         def multiply(c, w):
             b, row0, size = chunks[c]
@@ -196,16 +201,15 @@ def tile_multiheadselfattention_pa_t_kernel(
             if w == 0:
                 product = product_pool.tile([P, 2, 2 * BANK], F32)
                 products[c] = product
-            pairs = sums_of[c][w][:, 0:width].rearrange("p (n a) -> p n a", a=2)
-            for a, first_table in enumerate([COS, NEG_SIN]):
-                nc.vector.tensor_tensor(
-                    out=products[c][:, a, w * width : (w + 1) * width].rearrange(
-                        "p (n e) -> p n e", e=2
-                    ),
-                    in0=pairs[:, :, a : a + 1].to_broadcast([P, width // 2, 2]),
-                    in1=factors(first_table, row0, size),
-                    op=MULT,
-                )
+            sums = sums_of[c][w][:, 0:width].rearrange("p (n a) -> p a n", a=2)
+            nc.vector.tensor_tensor(
+                out=products[c][:, :, w * width : (w + 1) * width].rearrange(
+                    "p a (n e) -> p a n e", e=2
+                ),
+                in0=sums.unsqueeze(3).to_broadcast([P, 2, width // 2, 2]),
+                in1=factors(row0, size),
+                op=MULT,
+            )
 
         def new_output(c):
             rotated = out_pool.tile([P, 2 * BANK], F32, name="rotated")
@@ -270,7 +274,7 @@ def tile_multiheadselfattention_pa_t_kernel(
                 project(c - 1)
                 quantise(c, grouped)
                 if c in table_at:
-                    negate_sines(table_at[c])
+                    prepare_tables(table_at[c])
                 if c - 2 >= ON_VECTOR:
                     add_and_store(c - 2, nc.gpsimd)
                 rotate(c - 1)

@@ -25,7 +25,6 @@ ROWS = SEQ // P
 TILES = 4
 FIRST_SIZES = [1, 1, 2]
 AHEAD = 10
-ON_VECTOR = 2
 TOKEN = 8
 BANK = 512
 TABLE_ROWS = 4
@@ -41,14 +40,12 @@ FLOPS = 2 * BATCH * SEQ * D_MODEL * 2 * HEAD
 
 def chunk_list():
     chunks = []
-    for b in range(BATCH):
-        sizes = [TILES] * (ROWS // TILES)
-        if b == 0:
-            sizes = FIRST_SIZES + sizes[1:]
-        row = 0
-        for size in sizes:
-            chunks.append((b, row, size))
-            row += size
+    for first_row in range(0, ROWS, TILES):
+        for b in range(BATCH):
+            row = first_row
+            for size in FIRST_SIZES if not chunks else [TILES]:
+                chunks.append((b, row, size))
+                row += size
     return chunks
 
 
@@ -66,7 +63,7 @@ def tile_multiheadselfattention_pa_t_kernel(
         grouped_pool = stack.enter_context(tc.tile_pool(name="grouped", bufs=2))
         mx_pool = stack.enter_context(tc.tile_pool(name="mx", bufs=3))
         product_pool = stack.enter_context(tc.tile_pool(name="product", bufs=3))
-        out_pool = stack.enter_context(tc.tile_pool(name="out", bufs=6))
+        out_pool = stack.enter_context(tc.tile_pool(name="out", bufs=10))
         flipped_pool = stack.enter_context(tc.psum_pool(name="flipped", bufs=TILES))
         sums_pool = stack.enter_context(tc.psum_pool(name="sums", bufs=4))
 
@@ -242,7 +239,7 @@ def tile_multiheadselfattention_pa_t_kernel(
             multiply(c, 0)
             multiply(c, 1)
             new_output(c)
-            if c < ON_VECTOR or c == last:
+            if c == last:
                 add_and_store(c, nc.vector)
 
         with tc.manual_schedule():
@@ -256,26 +253,29 @@ def tile_multiheadselfattention_pa_t_kernel(
             load_x(3, 2, 4)
             load_x(4, 0, 2)
             load_x(4, 2, 4)
-            load_tables(1)
             load_x(5, 0, 2)
             load_x(5, 2, 4)
-            load_tables(2)
             load_x(6)
+            load_tables(1)
+            load_x(7)
+            load_x(8)
+            load_tables(2)
+            load_x(9)
             load_tables(3)
-            for c in range(7, AHEAD):
-                load_x(c)
 
-            table_at = {1: 0, 4: 1, 5: 2, 6: 3}
+            table_at = {1: 0}
+            for index in range(1, len(pieces)):
+                table_at[len(FIRST_SIZES) + BATCH * index - 2] = index
             quantise(0, transpose_and_group(0))
             for c in range(1, len(chunks)):
                 grouped = transpose_and_group(c)
-                if c - 2 >= ON_VECTOR:
+                if c >= 2:
                     mark_output(c - 2)
                 project(c - 1)
                 quantise(c, grouped)
                 if c in table_at:
                     prepare_tables(table_at[c])
-                if c - 2 >= ON_VECTOR:
+                if c >= 2:
                     add_and_store(c - 2, nc.gpsimd)
                 rotate(c - 1)
                 if c - 1 + AHEAD < len(chunks):

@@ -269,15 +269,20 @@ def tile_multiheadselfattention_pa_t_kernel(
             quantise(0, transpose_and_group(0))
             for c in range(1, len(chunks)):
                 grouped = transpose_and_group(c)
-                if c >= 2:
+                ready = [] if c == 1 else [0, 1] if c == 2 else [c - 1]
+                if c >= 3:
                     mark_output(c - 2)
-                project(c - 1)
+                for previous in ready:
+                    project(previous)
                 quantise(c, grouped)
                 if c in table_at:
                     prepare_tables(table_at[c])
-                if c >= 2:
+                if c >= 3:
                     add_and_store(c - 2, nc.gpsimd)
-                rotate(c - 1)
+                for previous in ready:
+                    rotate(previous)
+                    if previous == 0:
+                        add_and_store(0, nc.gpsimd)
                 if c - 1 + AHEAD < len(chunks):
                     load_x(c - 1 + AHEAD)
             project(last)

from contextlib import ExitStack

import concourse.mybir as mybir
from concourse.masks import make_identity

F32 = mybir.dt.float32
BF16 = mybir.dt.bfloat16
I32 = mybir.dt.int32
U32 = mybir.dt.uint32
U8 = mybir.dt.uint8
FP8X4 = mybir.dt.float8_e4m3fn_x4
FP4X4 = mybir.dt.float4_e2m1fn_x4
MULT = mybir.AluOpType.mult
ADD = mybir.AluOpType.add
COPY = mybir.ActivationFunctionType.Copy

P = 128
BATCH = 4
SEQ = 2048
D_MODEL = 1024
HEAD = 128
K_PASS = 4 * P
PASSES = D_MODEL // K_PASS
ROWS = SEQ // P
TILES = 4
FIRST_SIZES = [1, 1, 2]
AHEAD = 10
TOKEN = 8
BANK = 512
TABLE_ROWS = 4
PLANE = TABLE_ROWS * HEAD
COS = 0
SIN = 1
NEG_SIN = 2
COS_AGAIN = 3
SHIFT = 2

FLOPS = 2 * BATCH * SEQ * D_MODEL * 2 * HEAD


def chunk_list():
    chunks = []
    for first_row in range(0, ROWS, TILES):
        for b in range(BATCH):
            row = first_row
            for size in FIRST_SIZES if not chunks else [TILES]:
                chunks.append((b, row, size))
                row += size
    return chunks


def tile_multiheadselfattention_pa_t_kernel(
    tc, x, Wq_words, Wq_scales, Wk_words, Wk_scales, cos2, sin2, out_0, out_1
):
    nc = tc.nc
    outs = [out_0, out_1]
    chunks = chunk_list()
    last = len(chunks) - 1

    with ExitStack() as stack:
        const = stack.enter_context(tc.tile_pool(name="const", bufs=1))
        x_pool = stack.enter_context(tc.tile_pool(name="x", bufs=AHEAD))
        grouped_pool = stack.enter_context(tc.tile_pool(name="grouped", bufs=2))
        mx_pool = stack.enter_context(tc.tile_pool(name="mx", bufs=3))
        product_pool = stack.enter_context(tc.tile_pool(name="product", bufs=3))
        out_pool = stack.enter_context(tc.tile_pool(name="out", bufs=10))
        flipped_pool = stack.enter_context(tc.psum_pool(name="flipped", bufs=TILES))
        sums_pool = stack.enter_context(tc.psum_pool(name="sums", bufs=4))

        identity = const.tile([P, P], F32)
        make_identity(nc, identity[:])

        w_words = const.tile([P, 2, PASSES, 2 * HEAD], U8, align_bytes=64)
        w_planes = const.tile([P, 2, PASSES, HEAD], U8, align_bytes=64)
        nc.vector.memset(w_planes[:].rearrange("p w g n -> p (w g n)").bitcast(I32), 0)

        pieces = []
        for index in range(ROWS // TABLE_ROWS):
            table = const.tile([P, 4 * (PLANE + 1)], BF16, name="table%d" % index)
            pieces.append(table)

        x_tiles = {}
        codes_of = {}
        planes_of = {}
        sums_of = {}
        products = {}
        rotated_of = {}

        def load_x(c, first_tile=0, end_tile=None):
            b, row0, size = chunks[c]
            end_tile = end_tile or size
            if c not in x_tiles:
                x_sb = x_pool.tile([P, TILES, D_MODEL], BF16, name="x_sb")
                x_tiles[c] = x_sb
            rows = x[b].rearrange("(p t) k -> p t k", t=ROWS)
            nc.sync.dma_start(
                out=x_tiles[c][:, first_tile:end_tile, :],
                in_=rows[:, row0 + first_tile : row0 + end_tile, :],
            )

        def load_weight(w, words, scales):
            nc.sync.dma_start(
                out=w_words[:, w, :, :].bitcast(I32),
                in_=words.bitcast(I32).rearrange("g p c -> p g c"),
            )
            for quadrant in range(4):
                nc.sync.dma_start(
                    out=w_planes[32 * quadrant : 32 * quadrant + 4, w, :, :].bitcast(I32),
                    in_=scales.bitcast(I32)[:, 4 * quadrant : 4 * quadrant + 4, :].rearrange(
                        "g r n -> r g n"
                    ),
                )

        def load_tables(index):
            table = pieces[index]
            first = TABLE_ROWS * index
            for which, values in [(COS, cos2), (SIN, sin2)]:
                nc.sync.dma_start(
                    out=table[:, which * PLANE : (which + 1) * PLANE],
                    in_=values.rearrange("(p t) d -> p t d", t=ROWS)[
                        :, first : first + TABLE_ROWS, :
                    ].rearrange("p t d -> p (t d)"),
                )

        def prepare_tables(index):
            table = pieces[index]
            negated = table[:, NEG_SIN * PLANE + SHIFT : (NEG_SIN + 1) * PLANE + SHIFT]
            again = table[:, COS_AGAIN * PLANE + SHIFT : (COS_AGAIN + 1) * PLANE + SHIFT]
            sines = table[:, SIN * PLANE : (SIN + 1) * PLANE]
            cosines = table[:, COS * PLANE : (COS + 1) * PLANE]
            if index == 0:
                nc.vector.tensor_scalar_mul(out=negated, in0=sines, scalar1=-1.0)
                nc.vector.tensor_copy(out=again, in_=cosines)
            else:
                nc.scalar.activation(out=negated, in_=sines, func=COPY, scale=-1.0)
                nc.scalar.copy(out=again, in_=cosines)

        def transpose_and_group(c):
            size = chunks[c][2]
            grouped = grouped_pool.tile([P, TILES * D_MODEL], BF16, align_bytes=64)
            grouped_words = grouped[:].bitcast(F32)
            for i in range(size):
                words = x_tiles[c][:, i, :].bitcast(F32)
                flipped = flipped_pool.tile([P, BANK], F32)
                for g in range(PASSES):
                    for u in range(2):
                        nc.tensor.transpose(
                            flipped[:, (2 * g + u) * P : (2 * g + u + 1) * P],
                            words[:, 2 * P * g + u : 2 * P * (g + 1) : 2],
                            identity[:],
                        )
                nc.scalar.copy(
                    out=grouped_words[:, i * BANK : (i + 1) * BANK].rearrange(
                        "p (g r u) -> p g r u", g=PASSES, u=2
                    ),
                    in_=flipped[:].rearrange("p (g u r) -> p g r u", g=PASSES, u=2),
                )
            return grouped

        def quantise(c, grouped):
            size = chunks[c][2]
            codes = mx_pool.tile([P, TILES * PASSES * P], U32, align_bytes=64)
            planes = mx_pool.tile([P, TILES * PASSES * P], U8, align_bytes=64)
            nc.vector.quantize_mx(
                out=codes[:, 0 : size * PASSES * P].bitcast(FP8X4),
                scales=planes[:, 0 : size * PASSES * P],
                in_=grouped[:, 0 : size * D_MODEL],
            )
            codes_of[c] = codes
            planes_of[c] = planes

        def project(c):
            sums_of[c] = []
            for w in range(2):
                sums = sums_pool.tile([P, BANK], F32)
                for i in range(chunks[c][2]):
                    for g in range(PASSES):
                        tokens = slice((i * PASSES + g) * P, (i * PASSES + g + 1) * P)
                        nc.tensor.matmul_mx(
                            out=sums[:, i * HEAD : (i + 1) * HEAD],
                            lhsT=codes_of[c][:, tokens].bitcast(FP8X4),
                            lhsT_scale=planes_of[c][:, tokens],
                            rhs=w_words[:, w, g, :].bitcast(FP4X4),
                            rhs_scale=w_planes[:, w, g, :],
                            start=(g == 0),
                            stop=(g == PASSES - 1),
                        )
                sums_of[c].append(sums)

        def factors(row, size):
            place = row % TABLE_ROWS * HEAD
            rows = pieces[row // TABLE_ROWS][:].rearrange("p (a e n) -> p a e n", a=2, e=2)
            return rows[:, :, :, place : place + size * HEAD : 2].rearrange("p a e n -> p a n e")

        def multiply(c, w):
            b, row0, size = chunks[c]
            width = size * HEAD
            if w == 0:
                product = product_pool.tile([P, 2, 2 * BANK], F32)
                products[c] = product
            sums = sums_of[c][w][:, 0:width].rearrange("p (n a) -> p a n", a=2)
            nc.vector.tensor_tensor(
                out=products[c][:, :, w * width : (w + 1) * width].rearrange(
                    "p a (n e) -> p a n e", e=2
                ),
                in0=sums.unsqueeze(3).to_broadcast([P, 2, width // 2, 2]),
                in1=factors(row0, size),
                op=MULT,
            )

        def new_output(c):
            rotated = out_pool.tile([P, 2 * BANK], F32, name="rotated")
            rotated_of[c] = rotated

        def mark_output(c):
            nc.scalar.copy(out=rotated_of[c][:, 0:TOKEN], in_=identity[:, 0:TOKEN])

        def add_and_store(c, engine):
            b, row0, size = chunks[c]
            width = size * HEAD
            rotated = rotated_of[c]
            engine.tensor_tensor(
                out=rotated[:, 0 : 2 * width],
                in0=products[c][:, 0, 0 : 2 * width],
                in1=products[c][:, 1, 0 : 2 * width],
                op=ADD,
            )
            for w in range(2):
                nc.sync.dma_start(
                    out=outs[w][b, 0].rearrange("(p t) d -> p t d", t=ROWS)[
                        :, row0 : row0 + size, :
                    ],
                    in_=rotated[:, w * width : (w + 1) * width].rearrange(
                        "p (t d) -> p t d", d=HEAD
                    ),
                )

        def rotate(c):
            multiply(c, 0)
            multiply(c, 1)
            new_output(c)
            if c == last:
                add_and_store(c, nc.vector)

        with tc.manual_schedule():
            load_x(0)
            load_weight(0, Wq_words, Wq_scales)
            load_x(1)
            load_x(2)
            load_weight(1, Wk_words, Wk_scales)
            load_x(3, 0, 2)
            load_tables(0)
            load_x(3, 2, 4)
            load_x(4, 0, 2)
            load_x(4, 2, 4)
            load_x(5, 0, 2)
            load_x(5, 2, 4)
            load_x(6)
            load_tables(1)
            load_x(7)
            load_x(8)
            load_tables(2)
            load_x(9)
            load_tables(3)

            table_at = {1: 0}
            for index in range(1, len(pieces)):
                table_at[len(FIRST_SIZES) + BATCH * index - 2] = index
            quantise(0, transpose_and_group(0))
            for c in range(1, len(chunks)):
                grouped = transpose_and_group(c)
                ready = [] if c == 1 else [0, 1] if c == 2 else [c - 1]
                if c >= 3:
                    mark_output(c - 2)
                for previous in ready:
                    project(previous)
                quantise(c, grouped)
                if c in table_at:
                    prepare_tables(table_at[c])
                if c >= 3:
                    add_and_store(c - 2, nc.gpsimd)
                for previous in ready:
                    rotate(previous)
                    if previous == 0:
                        add_and_store(0, nc.gpsimd)
                if c - 1 + AHEAD < len(chunks):
                    load_x(c - 1 + AHEAD)
            project(last)
            add_and_store(last - 1, nc.gpsimd)
            rotate(last)
